import numpy as np
import ml_dtypes


def mxq(x, axis, fmt="e4m3"):
    dtype, down = {"e4m3": (ml_dtypes.float8_e4m3fn, 7), "e5m2": (ml_dtypes.float8_e5m2, 14)}[fmt]
    v = np.moveaxis(np.asarray(x, np.float32).astype(ml_dtypes.bfloat16).astype(np.float64), axis, -1)
    blocks = v.reshape(v.shape[:-1] + (-1, 32))
    amax = np.abs(blocks).max(-1, keepdims=True)
    byte = np.maximum(np.where(amax > 0, np.frexp(amax)[1] - 1 + 127, 0) - down, 1)
    scale = np.exp2(byte - 127.0)
    codes = (blocks / scale).astype(np.float32).astype(dtype).astype(np.float64)
    return np.moveaxis((codes * scale).reshape(v.shape), -1, axis)


WIDE = False


def mx_kscale(k):
    if not WIDE:
        return np.ones(k)
    levels = np.array([10, -10, 5, -5, 0])
    if k % 512:
        return np.exp2(np.random.permutation(np.resize(levels, k // 32))).repeat(32)
    a = np.empty((k // 512, 16))
    for p in range(k // 512):
        a[p, :8] = np.random.permutation(np.resize(levels, 8))
        for g in range(8):
            far = levels[np.abs(levels - a[p, g]) >= 10]
            a[p, g + 8] = far[np.random.randint(len(far))]
    return np.exp2(a.ravel()).repeat(32)


BF16 = ml_dtypes.bfloat16


def bf(x):
    return np.asarray(x, np.float32).astype(BF16)


def f64(x):
    return np.asarray(x).astype(np.float64)


E2M1 = np.array([0.0, 0.5, 1.0, 1.5, 2.0, 3.0, 4.0, 6.0, -0.0, -0.5, -1.0, -1.5, -2.0, -3.0, -4.0, -6.0])


def pack_weight(w, fmt):
    k, n = w.shape
    w = f64(bf(w)).reshape(k // 32, 32, n)
    amax = np.abs(w).max(1)
    if fmt == "e4m3":
        byte = np.frexp(amax)[1] - 1 + 127 - 7
    else:
        mant, ex = np.frexp(amax / 6.0)
        byte = np.where(mant > 0.5, ex, ex - 1) + 127
    byte = np.clip(np.where(amax > 0, byte, 1), 1, 254)
    scaled = (w * np.exp2(127.0 - byte)[:, None, :]).reshape(k, n).astype(np.float32)
    by_word = np.ascontiguousarray(scaled.reshape(k // 512, 128, 4, n).transpose(0, 1, 3, 2))
    if fmt == "e4m3":
        words = by_word.astype(ml_dtypes.float8_e4m3fn).view(np.uint8)
    else:
        c = by_word.astype(ml_dtypes.float4_e2m1fn).view(np.uint8) & 0xF
        words = c[..., 0::2] | (c[..., 1::2] << 4)
    return np.ascontiguousarray(words), np.ascontiguousarray(byte.astype(np.uint8).reshape(k // 512, 16, n))


def unpack_weight(words, scales, fmt):
    g, p, n, _ = words.shape
    if fmt == "e4m3":
        vals = np.ascontiguousarray(words).view(ml_dtypes.float8_e4m3fn).astype(np.float64)
    else:
        nib = np.empty((g, p, n, 4), np.uint8)
        nib[..., 0::2] = words & 0xF
        nib[..., 1::2] = words >> 4
        vals = E2M1[nib]
    vals = vals * np.repeat(np.exp2(scales.astype(np.float64) - 127.0), 8, axis=1)[..., None]
    return vals.transpose(0, 1, 3, 2).reshape(g * 512, n)
def pack4(w):
    words, scales = pack_weight(w, "e2m1")
    return words.reshape(words.shape[0], 128, -1), scales


def unpack4(words, scales):
    return unpack_weight(words.reshape(words.shape[0], 128, -1, 2), scales, "e2m1")


B, T, E, H, DK, C = 1, 1024, 1024, 4, 256, 512
DV = 2 * DK
F = H * DV
EPS = 1e-5


def draw0():
    s, t = mx_kscale(E), mx_kscale(F)
    o = np.random.standard_normal((B, T, H, DV)) * 5.0 * np.exp(0.5 * np.random.standard_normal((B, T, H, 1)))
    x = bf(np.random.standard_normal((B, T, E)) * s)
    Wg_words, Wg_scales = pack4(np.random.standard_normal((E, F)) / np.sqrt(E) / s[:, None] * t)
    gn_weight = bf(1.0 + 0.1 * np.random.standard_normal(DV))
    Wo_words, Wo_scales = pack4(np.random.standard_normal((F, E)) / np.sqrt(F) / t[:, None])
    return {"o_ret": bf(o),
            "x": x,
            "Wg_words": Wg_words,
            "Wg_scales": Wg_scales,
            "gn_weight": gn_weight,
            "Wo_words": Wo_words,
            "Wo_scales": Wo_scales}


def core(o_ret, x, Wg_words, Wg_scales, gn_weight, Wo_words, Wo_scales):
    o = f64(o_ret)
    rms = np.sqrt(np.mean(o * o, axis=-1, keepdims=True) + EPS)
    o = o / rms * f64(gn_weight)
    g = mxq(f64(x), 2, "e4m3") @ unpack4(Wg_words, Wg_scales)
    h = o.reshape(B, T, F) * g
    return mxq(h, 2, "e4m3") @ unpack4(Wo_words, Wo_scales)


def e4m3fn_bytes(y):
    return np.clip(np.asarray(y, np.float64), -448.0, 448.0).astype(np.float32).astype(ml_dtypes.float8_e4m3fn).view(np.uint8)


def e4m3fn_values(b):
    return np.asarray(b, np.uint8).view(ml_dtypes.float8_e4m3fn).astype(np.float64)


def setup_inputs():
    d = draw0()
    x0 = np.asarray(d['x']).astype(np.float64)
    s = (np.max(np.abs(x0), axis=(0, 1), keepdims=True) / 448.0).astype(np.float32)
    out = {}
    for k, v in d.items():
        if k == 'x':
            out['x_bytes'] = e4m3fn_bytes(x0 / s.astype(np.float64))
            out['x_scale'] = s
        else:
            out[k] = v
    return out


def reference(o_ret, x_bytes, x_scale, Wg_words, Wg_scales, gn_weight, Wo_words, Wo_scales):
    return core(o_ret, e4m3fn_values(x_bytes) * x_scale.astype(np.float64), Wg_words, Wg_scales, gn_weight, Wo_words, Wo_scales)

@@ -1,0 +1,270 @@
+from contextlib import ExitStack
+
+import concourse.mybir as mybir
+from concourse.masks import make_identity
+
+F32 = mybir.dt.float32
+BF16 = mybir.dt.bfloat16
+I32 = mybir.dt.int32
+U32 = mybir.dt.uint32
+U8 = mybir.dt.uint8
+E4M3 = mybir.dt.float8_e4m3fn
+FP8X4 = mybir.dt.float8_e4m3fn_x4
+FP4X4 = mybir.dt.float4_e2m1fn_x4
+ACT = mybir.ActivationFunctionType
+ALU = mybir.AluOpType
+
+T, E, H, DV = 1024, 1024, 4, 512
+F = H * DV
+P = 128
+NT = T // P
+GX = E // 512
+GH = F // 512
+EPS = 1e-5
+FLOPS = 2 * T * E * F * 2
+BYTES = T * F * 2 + T * E + E * 4 + 2 * (E * F // 2 + E * F // 32) + DV * 2 + T * E * 4
+
+
+def tile_multiscaleretention_pc_w4_kernel(
+    tc, o_ret, x_bytes, x_scale, Wg_words, Wg_scales, gn_weight, Wo_words, Wo_scales, out
+):
+    nc = tc.nc
+    o_view = o_ret.rearrange("b (p i) h d -> i p (b h d)", i=NT)
+    x_view = x_bytes.rearrange("b (p i) e -> p (b i) e", i=NT)
+    out_view = out.rearrange("b (p i) e -> i p (b e)", i=NT)
+
+    with ExitStack() as ctx:
+        const = ctx.enter_context(tc.tile_pool(name="const", bufs=1))
+        xpool = ctx.enter_context(tc.tile_pool(name="xpool", bufs=2))
+        hpool = ctx.enter_context(tc.tile_pool(name="hpool", bufs=2))
+        opool = ctx.enter_context(tc.tile_pool(name="opool", bufs=3))
+        psum = ctx.enter_context(tc.psum_pool(name="psum", bufs=8))
+
+        wg_sc = const.tile([P, GX, F], U8, name="wg_sc", align_bytes=64)
+        wo_sc = const.tile([P, GH, E], U8, name="wo_sc", align_bytes=64)
+        nc.vector.memset(wg_sc[:].rearrange("p g n -> p (g n)").bitcast(I32), 0)
+        ident = const.tile([P, P], F32, name="ident")
+        make_identity(nc, ident[:])
+        nc.gpsimd.memset(wo_sc[:].rearrange("p g n -> p (g n)").bitcast(I32), 0)
+
+        x_cuts = [(0, 1), (1, 4), (4, 8)]
+        x_tiles = [
+            const.tile([P, b - a, E], U8, name="xbytes%d" % a) for a, b in x_cuts
+        ]
+        o_tiles = [const.tile([P, F], BF16, name="o%d" % i) for i in range(NT)]
+        wg = [const.tile([P, GX, F], U8, name="wg%d" % k, align_bytes=64) for k in range(2)]
+        wo = [const.tile([P, 2, 2 * E], U8, name="wo%d" % k, align_bytes=64) for k in range(2)]
+        s4 = const.tile([P, GX, 4], F32, name="s4")
+        gnw = const.tile([P, DV], BF16, name="gnw")
+
+        def load_x(k):
+            a, b = x_cuts[k]
+            nc.sync.dma_start(out=x_tiles[k][:], in_=x_view[:, a:b, :])
+
+        def load_scales(sc, hbm):
+            for r in range(4):
+                nc.sync.dma_start(
+                    out=sc[r:P:32, :, :].rearrange("q g n -> q g n").bitcast(I32),
+                    in_=hbm[:, r:16:4, :].rearrange("g q n -> q g n").bitcast(I32),
+                )
+
+        def load_o(i):
+            nc.sync.dma_start(out=o_tiles[i][:], in_=o_view[i])
+
+        load_x(0)
+        nc.sync.dma_start(out=s4[:], in_=x_scale.rearrange("a b (g p t) -> p (a b g) t", p=P, t=4))
+        load_scales(wg_sc, Wg_scales)
+        wg_v = Wg_words.rearrange("g p n -> p g n")
+        nc.sync.dma_start(out=wg[0][:], in_=wg_v[:, :, 0:F])
+        load_o(0)
+        nc.sync.dma_start(out=gnw[:], in_=gn_weight.partition_broadcast(P))
+        nc.sync.dma_start(out=wg[1][:], in_=wg_v[:, :, F : 2 * F])
+        load_x(1)
+        load_o(1)
+        load_scales(wo_sc, Wo_scales)
+        wo_v = Wo_words.rearrange("g p n -> p g n")
+        nc.sync.dma_start(out=wo[0][:], in_=wo_v[:, 0:2, :])
+        nc.sync.dma_start(out=wo[1][:], in_=wo_v[:, 2:4, :])
+        load_o(2)
+        load_x(2)
+        for i in range(3, NT):
+            load_o(i)
+
+        xb, xs, xc, xsc = {}, {}, {}, {}
+        ss, rr, ow, hb, hs, hc, hsc = {}, {}, {}, {}, {}, {}, {}
+
+        def bank(name):
+            return psum.tile([P, 512], F32, name=name, tag="bank")
+
+        def x_src(i):
+            for k, (a, b) in enumerate(x_cuts):
+                if a <= i < b:
+                    return x_tiles[k][:, i - a, :]
+
+        def cast_x(i):
+            xb[i] = xpool.tile([P, E], BF16, name="xb", tag="xb", align_bytes=64)
+            src = x_src(i)
+            nc.scalar.copy(out=xb[i][:, 0:512], in_=src[:, 0:512].bitcast(E4M3))
+            nc.vector.tensor_copy(out=xb[i][:, 512:1024], in_=src[:, 512:1024].bitcast(E4M3))
+
+        def transpose_x(i):
+            b = bank("xt")
+            words = xb[i][:].bitcast(F32)
+            for g in range(GX):
+                for u in range(2):
+                    j = 2 * g + u
+                    nc.tensor.transpose(
+                        b[:, P * j : P * (j + 1)], words[:, 256 * g + u : 256 * (g + 1) : 2], ident[:]
+                    )
+            return b
+
+        def scale_x(i, b):
+            xs[i] = xpool.tile([P, GX, P, 4], BF16, name="xs", tag="xs", align_bytes=64)
+            for g in range(GX):
+                src = b[:, 256 * g : 256 * (g + 1)].bitcast(BF16)
+                nc.vector.tensor_tensor(
+                    out=xs[i][:, g].rearrange("p n (u e) -> p n u e", u=2),
+                    in0=src.rearrange("p (u n e) -> p n u e", u=2, e=2),
+                    in1=s4[:, g, :]
+                    .rearrange("p (u e) -> p u e", u=2)
+                    .unsqueeze(1)
+                    .to_broadcast([P, P, 2, 2]),
+                    op=ALU.mult,
+                )
+
+        def quant_x(i):
+            xc[i] = xpool.tile([P, GX * P], U32, name="xc", tag="xc", align_bytes=64)
+            xsc[i] = xpool.tile([P, GX * P], U8, name="xsc", tag="xsc", align_bytes=64)
+            nc.vector.quantize_mx(
+                out=xc[i][:].bitcast(FP8X4),
+                scales=xsc[i][:],
+                in_=xs[i][:].rearrange("p g n t -> p (g n t)"),
+            )
+
+        def stats(i):
+            ss[i] = hpool.tile([P, H], F32, name="ss", tag="ss")
+            for h in range(H):
+                junk = hpool.tile([P, DV], BF16, name="junk", tag="junk")
+                nc.scalar.activation(
+                    out=junk[:],
+                    in_=o_tiles[i][:, DV * h : DV * (h + 1)],
+                    func=ACT.Square,
+                    accum_out=ss[i][:, h : h + 1],
+                )
+            rms = hpool.tile([P, H], F32, name="rms", tag="rms")
+            nc.scalar.activation(out=rms[:], in_=ss[i][:], func=ACT.Sqrt, scale=1.0 / DV, bias=EPS)
+            ss[i] = rms
+
+        def recip(i):
+            rr[i] = hpool.tile([P, H], F32, name="rr", tag="rr")
+            nc.vector.reciprocal(out=rr[i][:], in_=ss[i][:])
+
+        def weigh_o(i, n_vector):
+            ow[i] = hpool.tile([P, F], F32, name="ow", tag="ow")
+            for h in range(H):
+                eng = nc.vector if h < n_vector else nc.gpsimd
+                cols = slice(DV * h, DV * (h + 1))
+                eng.tensor_tensor(out=ow[i][:, cols], in0=o_tiles[i][:, cols], in1=gnw[:], op=ALU.mult)
+
+        def gate(i):
+            hb[i] = hpool.tile([P, GH, 2, 256], BF16, name="hb", tag="hb", align_bytes=64)
+            for c in range(4):
+                b = bank("g")
+                wt = wg[c // 2]
+                n0 = 512 * (c % 2)
+                for g in range(GX):
+                    nc.tensor.matmul_mx(
+                        out=b[:],
+                        lhsT=xc[i][:, P * g : P * (g + 1)].bitcast(FP8X4),
+                        lhsT_scale=xsc[i][:, P * g : P * (g + 1)],
+                        rhs=wt[:, g, 2 * n0 : 2 * (n0 + 512)].bitcast(FP4X4),
+                        rhs_scale=wg_sc[:, g, 512 * c : 512 * (c + 1)],
+                        start=(g == 0),
+                        stop=(g == GX - 1),
+                    )
+                gv = b[:].rearrange("p (n u e) -> p u n e", u=2, e=2)
+                wv = ow[i][:, 512 * c : 512 * (c + 1)].rearrange("p (n u e) -> p u n e", u=2, e=2)
+                for u in range(2):
+                    nc.vector.scalar_tensor_tensor(
+                        out=hb[i][:, c, u].rearrange("p (n e) -> p n e", e=2),
+                        in0=gv[:, u],
+                        scalar=rr[i][:, c : c + 1],
+                        in1=wv[:, u],
+                        op0=ALU.mult,
+                        op1=ALU.mult,
+                    )
+
+        def transpose_h(i):
+            hs[i] = hpool.tile([P, GH, P, 4], BF16, name="hs", tag="hs", align_bytes=64)
+            words = hb[i][:].rearrange("p g u n -> p (g u n)").bitcast(F32)
+            dst = hs[i][:].rearrange("p g n t -> p (g n t)").bitcast(F32)
+            for half in range(2):
+                b = bank("ht")
+                for j in range(4):
+                    k = 4 * half + j
+                    nc.tensor.transpose(b[:, P * j : P * (j + 1)], words[:, P * k : P * (k + 1)], ident[:])
+                nc.scalar.copy(
+                    out=dst[:, 512 * half : 512 * (half + 1)].rearrange("p (g n u) -> p g n u", g=2, u=2),
+                    in_=b[:].rearrange("p (g u n) -> p g n u", g=2, u=2),
+                )
+
+        def quant_h(i):
+            hc[i] = hpool.tile([P, GH * P], U32, name="hc", tag="hc", align_bytes=64)
+            hsc[i] = hpool.tile([P, GH * P], U8, name="hsc", tag="hsc", align_bytes=64)
+            src = hs[i][:].rearrange("p g n t -> p (g n t)")
+            for half in range(2):
+                w = slice(256 * half, 256 * (half + 1))
+                nc.vector.quantize_mx(
+                    out=hc[i][:, w].bitcast(FP8X4),
+                    scales=hsc[i][:, w],
+                    in_=src[:, 1024 * half : 1024 * (half + 1)],
+                )
+
+        def project(i):
+            for n in range(2):
+                b = bank("acc")
+                for g in range(GH):
+                    nc.tensor.matmul_mx(
+                        out=b[:],
+                        lhsT=hc[i][:, P * g : P * (g + 1)].bitcast(FP8X4),
+                        lhsT_scale=hsc[i][:, P * g : P * (g + 1)],
+                        rhs=wo[g // 2][:, g % 2, E * n : E * (n + 1)].bitcast(FP4X4),
+                        rhs_scale=wo_sc[:, g, 512 * n : 512 * (n + 1)],
+                        start=(g == 0),
+                        stop=(g == GH - 1),
+                    )
+                res = opool.tile([P, 512], F32, name="res", tag="res")
+                nc.scalar.copy(out=res[:], in_=b[:])
+                nc.sync.dma_start(out=out_view[i][:, 512 * n : 512 * (n + 1)], in_=res[:])
+
+        with tc.manual_schedule():
+            for i in range(2):
+                cast_x(i)
+                b = transpose_x(i)
+                scale_x(i, b)
+                quant_x(i)
+            cast_x(2)
+            stats(0)
+            recip(0)
+            weigh_o(0, 2)
+            for k in range(-1, NT + 1):
+                if k + 1 < NT:
+                    gate(k + 1)
+                if k + 2 < NT:
+                    stats(k + 2)
+                    weigh_o(k + 2, 0)
+                if 0 <= k < NT:
+                    transpose_h(k)
+                if 2 <= k + 3 < NT:
+                    b = transpose_x(k + 3)
+                    scale_x(k + 3, b)
+                if 0 <= k < NT:
+                    quant_h(k)
+                if 2 <= k + 3 < NT:
+                    quant_x(k + 3)
+                if 3 <= k + 4 < NT:
+                    cast_x(k + 4)
+                if k + 2 < NT:
+                    recip(k + 2)
+                if 0 <= k - 1 < NT:
+                    project(k - 1)

@@ -21,6 +21,18 @@ NT = T // P
 GX = E // 512
 GH = F // 512
 EPS = 1e-5
+GCOLS = 256
+NVS = [1,1,1,1,1,1,1,1]
+GM1 = 4
+QX = 0
+VST = 4
+LA = 3
+SPOS = 9
+RPOS = 9
+CV = (0,)
+CH = (1,)
+SE = 1
+N1S = 1
 FLOPS = 2 * T * E * F * 2
 BYTES = T * F * 2 + T * E + E * 4 + 2 * (E * F // 2 + E * F // 32) + DV * 2 + T * E * 4
 
@@ -35,10 +47,11 @@ def tile_multiscaleretention_pc_w4_kernel(
 
     with ExitStack() as ctx:
         const = ctx.enter_context(tc.tile_pool(name="const", bufs=1))
-        xpool = ctx.enter_context(tc.tile_pool(name="xpool", bufs=2))
+        xpool = ctx.enter_context(tc.tile_pool(name="xpool", bufs=6))
         hpool = ctx.enter_context(tc.tile_pool(name="hpool", bufs=2))
         opool = ctx.enter_context(tc.tile_pool(name="opool", bufs=3))
-        psum = ctx.enter_context(tc.psum_pool(name="psum", bufs=8))
+        psum = ctx.enter_context(tc.psum_pool(name="psum", bufs=7))
+        wpsum = ctx.enter_context(tc.psum_pool(name="wpsum", bufs=1))
 
         wg_sc = const.tile([P, GX, F], U8, name="wg_sc", align_bytes=64)
         wo_sc = const.tile([P, GH, E], U8, name="wo_sc", align_bytes=64)
@@ -46,6 +59,8 @@ def tile_multiscaleretention_pc_w4_kernel(
         ident = const.tile([P, P], F32, name="ident")
         make_identity(nc, ident[:])
         nc.gpsimd.memset(wo_sc[:].rearrange("p g n -> p (g n)").bitcast(I32), 0)
+
+        ctx.enter_context(tc.manual_schedule())
 
         x_cuts = [(0, 1), (1, 4), (4, 8)]
         x_tiles = [
@@ -56,6 +71,9 @@ def tile_multiscaleretention_pc_w4_kernel(
         wo = [const.tile([P, 2, 2 * E], U8, name="wo%d" % k, align_bytes=64) for k in range(2)]
         s4 = const.tile([P, GX, 4], F32, name="s4")
         gnw = const.tile([P, DV], BF16, name="gnw")
+        w4 = const.tile([P, 4], BF16, name="w4")
+        identb = const.tile([P, P], BF16, name="identb")
+        nc.vector.tensor_copy(out=identb[:], in_=ident[:])
 
         def load_x(k):
             a, b = x_cuts[k]
@@ -71,22 +89,22 @@ def tile_multiscaleretention_pc_w4_kernel(
         def load_o(i):
             nc.sync.dma_start(out=o_tiles[i][:], in_=o_view[i])
 
+        wg_v = Wg_words.rearrange("g p n -> p g n")
+        wo_v = Wo_words.rearrange("g p n -> p g n")
         load_x(0)
         nc.sync.dma_start(out=s4[:], in_=x_scale.rearrange("a b (g p t) -> p (a b g) t", p=P, t=4))
+        nc.sync.dma_start(out=w4[:], in_=gn_weight.rearrange("(p t) -> p t", t=4))
+        load_x(1)
         load_scales(wg_sc, Wg_scales)
-        wg_v = Wg_words.rearrange("g p n -> p g n")
         nc.sync.dma_start(out=wg[0][:], in_=wg_v[:, :, 0:F])
         load_o(0)
-        nc.sync.dma_start(out=gnw[:], in_=gn_weight.partition_broadcast(P))
         nc.sync.dma_start(out=wg[1][:], in_=wg_v[:, :, F : 2 * F])
-        load_x(1)
         load_o(1)
+        load_x(2)
+        load_o(2)
         load_scales(wo_sc, Wo_scales)
-        wo_v = Wo_words.rearrange("g p n -> p g n")
         nc.sync.dma_start(out=wo[0][:], in_=wo_v[:, 0:2, :])
         nc.sync.dma_start(out=wo[1][:], in_=wo_v[:, 2:4, :])
-        load_o(2)
-        load_x(2)
         for i in range(3, NT):
             load_o(i)
 
@@ -105,7 +123,10 @@ def tile_multiscaleretention_pc_w4_kernel(
             xb[i] = xpool.tile([P, E], BF16, name="xb", tag="xb", align_bytes=64)
             src = x_src(i)
             nc.scalar.copy(out=xb[i][:, 0:512], in_=src[:, 0:512].bitcast(E4M3))
-            nc.vector.tensor_copy(out=xb[i][:, 512:1024], in_=src[:, 512:1024].bitcast(E4M3))
+            if i not in CV:
+                nc.scalar.copy(out=xb[i][:, 512:1024], in_=src[:, 512:1024].bitcast(E4M3))
+            else:
+                nc.vector.tensor_copy(out=xb[i][:, 512:1024], in_=src[:, 512:1024].bitcast(E4M3))
 
         def transpose_x(i):
             b = bank("xt")
@@ -118,9 +139,10 @@ def tile_multiscaleretention_pc_w4_kernel(
                     )
             return b
 
-        def scale_x(i, b):
-            xs[i] = xpool.tile([P, GX, P, 4], BF16, name="xs", tag="xs", align_bytes=64)
-            for g in range(GX):
+        def scale_x(i, b, passes):
+            if passes[0] == 0:
+                xs[i] = xpool.tile([P, GX, P, 4], BF16, name="xs", tag="xs", align_bytes=64)
+            for g in passes:
                 src = b[:, 256 * g : 256 * (g + 1)].bitcast(BF16)
                 nc.vector.tensor_tensor(
                     out=xs[i][:, g].rearrange("p n (u e) -> p n u e", u=2),
@@ -132,25 +154,38 @@ def tile_multiscaleretention_pc_w4_kernel(
                     op=ALU.mult,
                 )
 
-        def quant_x(i):
-            xc[i] = xpool.tile([P, GX * P], U32, name="xc", tag="xc", align_bytes=64)
-            xsc[i] = xpool.tile([P, GX * P], U8, name="xsc", tag="xsc", align_bytes=64)
+        def quant_x(i, passes):
+            if passes[0] == 0:
+                xc[i] = xpool.tile([P, GX * P], U32, name="xc", tag="xc", align_bytes=64)
+                xsc[i] = xpool.tile([P, GX * P], U8, name="xsc", tag="xsc", align_bytes=64)
+            w = slice(P * passes[0], P * (passes[-1] + 1))
             nc.vector.quantize_mx(
-                out=xc[i][:].bitcast(FP8X4),
-                scales=xsc[i][:],
-                in_=xs[i][:].rearrange("p g n t -> p (g n t)"),
+                out=xc[i][:, w].bitcast(FP8X4),
+                scales=xsc[i][:, w],
+                in_=xs[i][:, passes[0] : passes[-1] + 1].rearrange("p g n t -> p (g n t)"),
             )
 
         def stats(i):
             ss[i] = hpool.tile([P, H], F32, name="ss", tag="ss")
+            sv = hpool.tile([P, H], F32, name="sv", tag="sv")
             for h in range(H):
-                junk = hpool.tile([P, DV], BF16, name="junk", tag="junk")
-                nc.scalar.activation(
-                    out=junk[:],
-                    in_=o_tiles[i][:, DV * h : DV * (h + 1)],
-                    func=ACT.Square,
-                    accum_out=ss[i][:, h : h + 1],
-                )
+                src = o_tiles[i][:, DV * h : DV * (h + 1)]
+                if i == 0 and h >= VST:
+                    vjunk = hpool.tile([P, DV], BF16, name="vjunk", tag="vjunk")
+                    nc.vector.scalar_tensor_tensor(
+                        out=vjunk[:], in0=src, scalar=1.0, in1=src, op0=ALU.mult, op1=ALU.mult,
+                        accum_out=sv[:, h : h + 1],
+                    )
+                else:
+                    junk = hpool.tile([P, DV], BF16, name="junk", tag="junk")
+                    nc.scalar.activation(out=junk[:], in_=src, func=ACT.Square, accum_out=ss[i][:, h : h + 1])
+            if i == 0:
+                rms = hpool.tile([P, H], F32, name="rms", tag="rms")
+                nc.scalar.activation(out=rms[:, 0:VST], in_=ss[i][:, 0:VST], func=ACT.Sqrt, scale=1.0 / DV, bias=EPS)
+                if VST < 4:
+                    nc.scalar.activation(out=rms[:, VST:4], in_=sv[:, VST:4], func=ACT.Sqrt, scale=1.0 / DV, bias=EPS)
+                ss[i] = rms
+                return
             rms = hpool.tile([P, H], F32, name="rms", tag="rms")
             nc.scalar.activation(out=rms[:], in_=ss[i][:], func=ACT.Sqrt, scale=1.0 / DV, bias=EPS)
             ss[i] = rms
@@ -159,40 +194,65 @@ def tile_multiscaleretention_pc_w4_kernel(
             rr[i] = hpool.tile([P, H], F32, name="rr", tag="rr")
             nc.vector.reciprocal(out=rr[i][:], in_=ss[i][:])
 
+        wb = wpsum.tile([P, DV], BF16, name="wb")
+
+        def spread_w():
+            for t in range(4):
+                nc.tensor.transpose(
+                    wb[:, P * t : P * (t + 1)], w4[:, t : t + 1].to_broadcast([P, P]), identb[:]
+                )
+            nc.scalar.copy(
+                out=gnw[:].rearrange("p (n t) -> p n t", t=4),
+                in_=wb[:].rearrange("p (t n) -> p n t", t=4),
+            )
+
         def weigh_o(i, n_vector):
             ow[i] = hpool.tile([P, F], F32, name="ow", tag="ow")
-            for h in range(H):
-                eng = nc.vector if h < n_vector else nc.gpsimd
+            for h in range(n_vector):
                 cols = slice(DV * h, DV * (h + 1))
-                eng.tensor_tensor(out=ow[i][:, cols], in0=o_tiles[i][:, cols], in1=gnw[:], op=ALU.mult)
+                nc.vector.tensor_tensor(
+                    out=ow[i][:, cols].rearrange("p (n t) -> p n t", t=4),
+                    in0=o_tiles[i][:, cols].rearrange("p (n t) -> p n t", t=4),
+                    in1=wb[:].rearrange("p (t n) -> p n t", t=4),
+                    op=ALU.mult,
+                )
+            for a in range(DV * n_vector, F, GCOLS):
+                cols = slice(a, a + GCOLS)
+                wcols = slice(a % DV, a % DV + GCOLS)
+                nc.gpsimd.tensor_tensor(
+                    out=ow[i][:, cols], in0=o_tiles[i][:, cols], in1=gnw[:, wcols], op=ALU.mult
+                )
 
-        def gate(i):
-            hb[i] = hpool.tile([P, GH, 2, 256], BF16, name="hb", tag="hb", align_bytes=64)
-            for c in range(4):
-                b = bank("g")
-                wt = wg[c // 2]
-                n0 = 512 * (c % 2)
-                for g in range(GX):
-                    nc.tensor.matmul_mx(
-                        out=b[:],
-                        lhsT=xc[i][:, P * g : P * (g + 1)].bitcast(FP8X4),
-                        lhsT_scale=xsc[i][:, P * g : P * (g + 1)],
-                        rhs=wt[:, g, 2 * n0 : 2 * (n0 + 512)].bitcast(FP4X4),
-                        rhs_scale=wg_sc[:, g, 512 * c : 512 * (c + 1)],
-                        start=(g == 0),
-                        stop=(g == GX - 1),
-                    )
-                gv = b[:].rearrange("p (n u e) -> p u n e", u=2, e=2)
-                wv = ow[i][:, 512 * c : 512 * (c + 1)].rearrange("p (n u e) -> p u n e", u=2, e=2)
-                for u in range(2):
-                    nc.vector.scalar_tensor_tensor(
-                        out=hb[i][:, c, u].rearrange("p (n e) -> p n e", e=2),
-                        in0=gv[:, u],
-                        scalar=rr[i][:, c : c + 1],
-                        in1=wv[:, u],
-                        op0=ALU.mult,
-                        op1=ALU.mult,
-                    )
+        gb = {}
+
+        def gate_mm(i, order):
+            for c, g in order:
+                if g == 0:
+                    gb[i, c] = bank("g")
+                nc.tensor.matmul_mx(
+                    out=gb[i, c][:],
+                    lhsT=xc[i][:, P * g : P * (g + 1)].bitcast(FP8X4),
+                    lhsT_scale=xsc[i][:, P * g : P * (g + 1)],
+                    rhs=wg[c // 2][:, g, 1024 * (c % 2) : 1024 * (c % 2) + 1024].bitcast(FP4X4),
+                    rhs_scale=wg_sc[:, g, 512 * c : 512 * (c + 1)],
+                    start=(g == 0),
+                    stop=(g == GX - 1),
+                )
+
+        def gate_mul(i, c):
+            if c == 0:
+                hb[i] = hpool.tile([P, GH, 2, 256], BF16, name="hb", tag="hb", align_bytes=64)
+            gv = gb[i, c][:].rearrange("p (n u e) -> p u n e", u=2, e=2)
+            wv = ow[i][:, 512 * c : 512 * (c + 1)].rearrange("p (n u e) -> p u n e", u=2, e=2)
+            for u in range(2):
+                nc.vector.scalar_tensor_tensor(
+                    out=hb[i][:, c, u].rearrange("p (n e) -> p n e", e=2),
+                    in0=gv[:, u],
+                    scalar=rr[i][:, c : c + 1],
+                    in1=wv[:, u],
+                    op0=ALU.mult,
+                    op1=ALU.mult,
+                )
 
         def transpose_h(i):
             hs[i] = hpool.tile([P, GH, P, 4], BF16, name="hs", tag="hs", align_bytes=64)
@@ -211,60 +271,106 @@ def tile_multiscaleretention_pc_w4_kernel(
         def quant_h(i):
             hc[i] = hpool.tile([P, GH * P], U32, name="hc", tag="hc", align_bytes=64)
             hsc[i] = hpool.tile([P, GH * P], U8, name="hsc", tag="hsc", align_bytes=64)
-            src = hs[i][:].rearrange("p g n t -> p (g n t)")
-            for half in range(2):
-                w = slice(256 * half, 256 * (half + 1))
-                nc.vector.quantize_mx(
-                    out=hc[i][:, w].bitcast(FP8X4),
-                    scales=hsc[i][:, w],
-                    in_=src[:, 1024 * half : 1024 * (half + 1)],
+            nc.vector.quantize_mx(
+                out=hc[i][:].bitcast(FP8X4),
+                scales=hsc[i][:],
+                in_=hs[i][:].rearrange("p g n t -> p (g n t)"),
+            )
+
+        acc = {}
+
+        def project_mm(i, n):
+            acc[i, n] = bank("acc")
+            for g in range(GH):
+                nc.tensor.matmul_mx(
+                    out=acc[i, n][:],
+                    lhsT=hc[i][:, P * g : P * (g + 1)].bitcast(FP8X4),
+                    lhsT_scale=hsc[i][:, P * g : P * (g + 1)],
+                    rhs=wo[g // 2][:, g % 2, E * n : E * (n + 1)].bitcast(FP4X4),
+                    rhs_scale=wo_sc[:, g, 512 * n : 512 * (n + 1)],
+                    start=(g == 0),
+                    stop=(g == GH - 1),
                 )
 
-        def project(i):
-            for n in range(2):
-                b = bank("acc")
-                for g in range(GH):
-                    nc.tensor.matmul_mx(
-                        out=b[:],
-                        lhsT=hc[i][:, P * g : P * (g + 1)].bitcast(FP8X4),
-                        lhsT_scale=hsc[i][:, P * g : P * (g + 1)],
-                        rhs=wo[g // 2][:, g % 2, E * n : E * (n + 1)].bitcast(FP4X4),
-                        rhs_scale=wo_sc[:, g, 512 * n : 512 * (n + 1)],
-                        start=(g == 0),
-                        stop=(g == GH - 1),
-                    )
-                res = opool.tile([P, 512], F32, name="res", tag="res")
+        def store(i, n):
+            b = acc[i, n]
+            res = opool.tile([P, 512], F32, name="res%d" % n, tag="res%d" % n)
+            if n == 0 or (N1S and i < NT - 1):
                 nc.scalar.copy(out=res[:], in_=b[:])
-                nc.sync.dma_start(out=out_view[i][:, 512 * n : 512 * (n + 1)], in_=res[:])
+            elif i == NT - 1:
+                nc.scalar.copy(out=res[:, 0:256], in_=b[:, 0:256])
+                nc.vector.tensor_copy(out=res[:, 256:512], in_=b[:, 256:512])
+            else:
+                nc.vector.tensor_copy(out=res[:], in_=b[:])
+            nc.sync.dma_start(out=out_view[i][:, 512 * n : 512 * (n + 1)], in_=res[:])
 
-        with tc.manual_schedule():
-            for i in range(2):
-                cast_x(i)
-                b = transpose_x(i)
-                scale_x(i, b)
-                quant_x(i)
-            cast_x(2)
+        by_bank = [(c, g) for c in range(4) for g in range(GX)]
+        by_pass = [(c, g) for g in range(GX) for c in range(4)]
+
+        cast_x(0)
+        b = transpose_x(0)
+        for g in range(GX):
+            scale_x(0, b, [g])
+            quant_x(0, [g])
+        spread_w()
+        cast_x(1)
+        b = transpose_x(1)
+        scale_x(1, b, [0, 1])
+        quant_x(1, [0, 1])
+        gate_mm(0, by_bank[:4])
+        for i in range(2, LA):
+            cast_x(i)
+            b = transpose_x(i)
+            if i == SPOS:
+                stats(0)
+                weigh_o(0, NVS[0])
+            if i == RPOS:
+                recip(0)
+            scale_x(i, b, [0, 1])
+            quant_x(i, [0, 1])
+            if i == 2:
+                gate_mm(0, by_bank[4:])
+        if SPOS >= LA:
             stats(0)
+            weigh_o(0, NVS[0])
+        if RPOS >= LA:
             recip(0)
-            weigh_o(0, 2)
-            for k in range(-1, NT + 1):
-                if k + 1 < NT:
-                    gate(k + 1)
-                if k + 2 < NT:
-                    stats(k + 2)
-                    weigh_o(k + 2, 0)
-                if 0 <= k < NT:
-                    transpose_h(k)
-                if 2 <= k + 3 < NT:
-                    b = transpose_x(k + 3)
-                    scale_x(k + 3, b)
-                if 0 <= k < NT:
-                    quant_h(k)
-                if 2 <= k + 3 < NT:
-                    quant_x(k + 3)
-                if 3 <= k + 4 < NT:
-                    cast_x(k + 4)
-                if k + 2 < NT:
-                    recip(k + 2)
-                if 0 <= k - 1 < NT:
-                    project(k - 1)
+        gate_mm(1, by_bank[:GM1])
+        for c in range(4):
+            gate_mul(0, c)
+        stats(1)
+        weigh_o(1, NVS[1])
+        cast_x(LA)
+        recip(1)
+        for k in range(0, NT + 1):
+            if 0 <= k - 2 < NT:
+                store(k - 2, 1)
+            if k + 1 < NT:
+                gate_mm(k + 1, by_bank[GM1:] if k == 0 else by_bank)
+                for c in range(4):
+                    gate_mul(k + 1, c)
+            if 0 <= k < NT and k < SE:
+                transpose_h(k)
+            if k + 2 < NT:
+                stats(k + 2)
+                weigh_o(k + 2, NVS[k + 2])
+            if 0 <= k < NT and k >= SE:
+                transpose_h(k)
+            if k + LA < NT:
+                bx = transpose_x(k + LA)
+                scale_x(k + LA, bx, [0, 1])
+                if QX:
+                    quant_x(k + LA, [0, 1])
+            if 0 <= k < NT:
+                quant_h(k)
+            if k + LA < NT and not QX:
+                quant_x(k + LA, [0, 1])
+            if k + LA + 1 < NT:
+                cast_x(k + LA + 1)
+            if k + 2 < NT:
+                recip(k + 2)
+            if 0 <= k - 1 < NT:
+                project_mm(k - 1, 0)
+                store(k - 1, 0)
+                project_mm(k - 1, 1)
+        store(NT - 1, 1)

@@ -25,11 +25,10 @@ GCOLS = 256
 NVS = [1,1,1,1,1,1,1,1]
 GM1 = 4
 QX = 0
-VST = 4
 LA = 3
 SPOS = 9
 RPOS = 9
-CV = (0,)
+CV = range(8)
 CH = (1,)
 SE = 1
 N1S = 1
@@ -48,7 +47,7 @@ def tile_multiscaleretention_pc_w4_kernel(
     with ExitStack() as ctx:
         const = ctx.enter_context(tc.tile_pool(name="const", bufs=1))
         xpool = ctx.enter_context(tc.tile_pool(name="xpool", bufs=6))
-        hpool = ctx.enter_context(tc.tile_pool(name="hpool", bufs=2))
+        hpool = ctx.enter_context(tc.tile_pool(name="hpool", bufs=3))
         opool = ctx.enter_context(tc.tile_pool(name="opool", bufs=3))
         psum = ctx.enter_context(tc.psum_pool(name="psum", bufs=7))
         wpsum = ctx.enter_context(tc.psum_pool(name="wpsum", bufs=1))
@@ -58,7 +57,7 @@ def tile_multiscaleretention_pc_w4_kernel(
         nc.vector.memset(wg_sc[:].rearrange("p g n -> p (g n)").bitcast(I32), 0)
         ident = const.tile([P, P], F32, name="ident")
         make_identity(nc, ident[:])
-        nc.gpsimd.memset(wo_sc[:].rearrange("p g n -> p (g n)").bitcast(I32), 0)
+        nc.vector.memset(wo_sc[:].rearrange("p g n -> p (g n)").bitcast(I32), 0)
 
         ctx.enter_context(tc.manual_schedule())
 
@@ -91,13 +90,15 @@ def tile_multiscaleretention_pc_w4_kernel(
 
         wg_v = Wg_words.rearrange("g p n -> p g n")
         wo_v = Wo_words.rearrange("g p n -> p g n")
+        wg_v = Wg_words.rearrange("g p n -> p g n")
+        wo_v = Wo_words.rearrange("g p n -> p g n")
         load_x(0)
         nc.sync.dma_start(out=s4[:], in_=x_scale.rearrange("a b (g p t) -> p (a b g) t", p=P, t=4))
         nc.sync.dma_start(out=w4[:], in_=gn_weight.rearrange("(p t) -> p t", t=4))
         load_x(1)
+        load_o(0)
         load_scales(wg_sc, Wg_scales)
         nc.sync.dma_start(out=wg[0][:], in_=wg_v[:, :, 0:F])
-        load_o(0)
         nc.sync.dma_start(out=wg[1][:], in_=wg_v[:, :, F : 2 * F])
         load_o(1)
         load_x(2)
@@ -105,8 +106,11 @@ def tile_multiscaleretention_pc_w4_kernel(
         load_scales(wo_sc, Wo_scales)
         nc.sync.dma_start(out=wo[0][:], in_=wo_v[:, 0:2, :])
         nc.sync.dma_start(out=wo[1][:], in_=wo_v[:, 2:4, :])
-        for i in range(3, NT):
-            load_o(i)
+        load_o(3)
+        load_o(4)
+        load_o(5)
+        load_o(6)
+        load_o(7)
 
         xb, xs, xc, xsc = {}, {}, {}, {}
         ss, rr, ow, hb, hs, hc, hsc = {}, {}, {}, {}, {}, {}, {}
@@ -133,7 +137,7 @@ def tile_multiscaleretention_pc_w4_kernel(
             words = xb[i][:].bitcast(F32)
             for g in range(GX):
                 for u in range(2):
-                    j = 2 * g + u
+                    j = 2 * u + g
                     nc.tensor.transpose(
                         b[:, P * j : P * (j + 1)], words[:, 256 * g + u : 256 * (g + 1) : 2], ident[:]
                     )
@@ -142,17 +146,17 @@ def tile_multiscaleretention_pc_w4_kernel(
         def scale_x(i, b, passes):
             if passes[0] == 0:
                 xs[i] = xpool.tile([P, GX, P, 4], BF16, name="xs", tag="xs", align_bytes=64)
-            for g in passes:
-                src = b[:, 256 * g : 256 * (g + 1)].bitcast(BF16)
-                nc.vector.tensor_tensor(
-                    out=xs[i][:, g].rearrange("p n (u e) -> p n u e", u=2),
-                    in0=src.rearrange("p (u n e) -> p n u e", u=2, e=2),
-                    in1=s4[:, g, :]
-                    .rearrange("p (u e) -> p u e", u=2)
-                    .unsqueeze(1)
-                    .to_broadcast([P, P, 2, 2]),
-                    op=ALU.mult,
-                )
+            g0, g1 = passes[0], passes[-1] + 1
+            src = b[:].bitcast(BF16).rearrange("p (u g n e) -> p g n u e", u=2, g=GX, e=2)
+            nc.vector.tensor_tensor(
+                out=xs[i][:, g0:g1].rearrange("p g n (u e) -> p g n u e", u=2),
+                in0=src[:, g0:g1],
+                in1=s4[:, g0:g1, :]
+                .rearrange("p g (u e) -> p g u e", u=2)
+                .unsqueeze(2)
+                .to_broadcast([P, g1 - g0, P, 2, 2]),
+                op=ALU.mult,
+            )
 
         def quant_x(i, passes):
             if passes[0] == 0:
@@ -167,32 +171,17 @@ def tile_multiscaleretention_pc_w4_kernel(
 
         def stats(i):
             ss[i] = hpool.tile([P, H], F32, name="ss", tag="ss")
-            sv = hpool.tile([P, H], F32, name="sv", tag="sv")
             for h in range(H):
                 src = o_tiles[i][:, DV * h : DV * (h + 1)]
-                if i == 0 and h >= VST:
-                    vjunk = hpool.tile([P, DV], BF16, name="vjunk", tag="vjunk")
-                    nc.vector.scalar_tensor_tensor(
-                        out=vjunk[:], in0=src, scalar=1.0, in1=src, op0=ALU.mult, op1=ALU.mult,
-                        accum_out=sv[:, h : h + 1],
-                    )
-                else:
-                    junk = hpool.tile([P, DV], BF16, name="junk", tag="junk")
-                    nc.scalar.activation(out=junk[:], in_=src, func=ACT.Square, accum_out=ss[i][:, h : h + 1])
-            if i == 0:
-                rms = hpool.tile([P, H], F32, name="rms", tag="rms")
-                nc.scalar.activation(out=rms[:, 0:VST], in_=ss[i][:, 0:VST], func=ACT.Sqrt, scale=1.0 / DV, bias=EPS)
-                if VST < 4:
-                    nc.scalar.activation(out=rms[:, VST:4], in_=sv[:, VST:4], func=ACT.Sqrt, scale=1.0 / DV, bias=EPS)
-                ss[i] = rms
-                return
-            rms = hpool.tile([P, H], F32, name="rms", tag="rms")
-            nc.scalar.activation(out=rms[:], in_=ss[i][:], func=ACT.Sqrt, scale=1.0 / DV, bias=EPS)
-            ss[i] = rms
+                junk = hpool.tile([P, DV], BF16, name="junk", tag="junk")
+                nc.scalar.activation(out=junk[:], in_=src, func=ACT.Square, accum_out=ss[i][:, h : h + 1])
+            rr[i] = hpool.tile([P, H], F32, name="rr", tag="rr")
+            nc.scalar.activation(
+                out=rr[i][:], in_=ss[i][:], func=ACT.Abs_reciprocal_sqrt, scale=1.0 / DV, bias=EPS
+            )
 
         def recip(i):
-            rr[i] = hpool.tile([P, H], F32, name="rr", tag="rr")
-            nc.vector.reciprocal(out=rr[i][:], in_=ss[i][:])
+            pass
 
         wb = wpsum.tile([P, DV], BF16, name="wb")
 
@@ -317,30 +306,21 @@ def tile_multiscaleretention_pc_w4_kernel(
         b = transpose_x(1)
         scale_x(1, b, [0, 1])
         quant_x(1, [0, 1])
+        stats(0)
+        weigh_o(0, NVS[0])
+        recip(0)
         gate_mm(0, by_bank[:4])
-        for i in range(2, LA):
-            cast_x(i)
-            b = transpose_x(i)
-            if i == SPOS:
-                stats(0)
-                weigh_o(0, NVS[0])
-            if i == RPOS:
-                recip(0)
-            scale_x(i, b, [0, 1])
-            quant_x(i, [0, 1])
-            if i == 2:
-                gate_mm(0, by_bank[4:])
-        if SPOS >= LA:
-            stats(0)
-            weigh_o(0, NVS[0])
-        if RPOS >= LA:
-            recip(0)
+        cast_x(2)
+        gate_mm(0, by_bank[4:])
+        b = transpose_x(2)
         gate_mm(1, by_bank[:GM1])
         for c in range(4):
             gate_mul(0, c)
         stats(1)
         weigh_o(1, NVS[1])
-        cast_x(LA)
+        scale_x(2, b, [0, 1])
+        quant_x(2, [0, 1])
+        cast_x(3)
         recip(1)
         for k in range(0, NT + 1):
             if 0 <= k - 2 < NT:

@@ -28,10 +28,12 @@ QX = 0
 LA = 3
 SPOS = 9
 RPOS = 9
-CV = range(8)
+CV = (0,)
 CH = (1,)
 SE = 1
 N1S = 1
+GHS = 1
+GH1 = 1
 FLOPS = 2 * T * E * F * 2
 BYTES = T * F * 2 + T * E + E * 4 + 2 * (E * F // 2 + E * F // 32) + DV * 2 + T * E * 4
 
@@ -47,7 +49,7 @@ def tile_multiscaleretention_pc_w4_kernel(
     with ExitStack() as ctx:
         const = ctx.enter_context(tc.tile_pool(name="const", bufs=1))
         xpool = ctx.enter_context(tc.tile_pool(name="xpool", bufs=6))
-        hpool = ctx.enter_context(tc.tile_pool(name="hpool", bufs=3))
+        hpool = ctx.enter_context(tc.tile_pool(name="hpool", bufs=2))
         opool = ctx.enter_context(tc.tile_pool(name="opool", bufs=3))
         psum = ctx.enter_context(tc.psum_pool(name="psum", bufs=7))
         wpsum = ctx.enter_context(tc.psum_pool(name="wpsum", bufs=1))
@@ -96,9 +98,9 @@ def tile_multiscaleretention_pc_w4_kernel(
         nc.sync.dma_start(out=s4[:], in_=x_scale.rearrange("a b (g p t) -> p (a b g) t", p=P, t=4))
         nc.sync.dma_start(out=w4[:], in_=gn_weight.rearrange("(p t) -> p t", t=4))
         load_x(1)
-        load_o(0)
         load_scales(wg_sc, Wg_scales)
         nc.sync.dma_start(out=wg[0][:], in_=wg_v[:, :, 0:F])
+        load_o(0)
         nc.sync.dma_start(out=wg[1][:], in_=wg_v[:, :, F : 2 * F])
         load_o(1)
         load_x(2)
@@ -195,8 +197,12 @@ def tile_multiscaleretention_pc_w4_kernel(
                 in_=wb[:].rearrange("p (t n) -> p n t", t=4),
             )
 
-        def weigh_o(i, n_vector):
-            ow[i] = hpool.tile([P, F], F32, name="ow", tag="ow")
+        def alloc_ow(i):
+            if i not in ow:
+                ow[i] = opool.tile([P, F], F32, name="ow", tag="ow")
+
+        def weigh_o_v(i, n_vector):
+            alloc_ow(i)
             for h in range(n_vector):
                 cols = slice(DV * h, DV * (h + 1))
                 nc.vector.tensor_tensor(
@@ -205,12 +211,22 @@ def tile_multiscaleretention_pc_w4_kernel(
                     in1=wb[:].rearrange("p (t n) -> p n t", t=4),
                     op=ALU.mult,
                 )
-            for a in range(DV * n_vector, F, GCOLS):
-                cols = slice(a, a + GCOLS)
-                wcols = slice(a % DV, a % DV + GCOLS)
+
+        def weigh_o_g(i, n_vector, heads):
+            alloc_ow(i)
+            for h in range(n_vector, H, heads):
+                n = min(heads, H - h)
+                cols = slice(DV * h, DV * (h + n))
                 nc.gpsimd.tensor_tensor(
-                    out=ow[i][:, cols], in0=o_tiles[i][:, cols], in1=gnw[:, wcols], op=ALU.mult
+                    out=ow[i][:, cols],
+                    in0=o_tiles[i][:, cols],
+                    in1=gnw[:],
+                    op=ALU.mult,
                 )
+
+        def after(tile):
+            token = hpool.tile([P, 1], U32, name="token", tag="token")
+            nc.gpsimd.tensor_copy(out=token[:], in_=tile[:, 0:1])
 
         gb = {}
 
@@ -306,22 +322,25 @@ def tile_multiscaleretention_pc_w4_kernel(
         b = transpose_x(1)
         scale_x(1, b, [0, 1])
         quant_x(1, [0, 1])
-        stats(0)
-        weigh_o(0, NVS[0])
-        recip(0)
         gate_mm(0, by_bank[:4])
         cast_x(2)
-        gate_mm(0, by_bank[4:])
         b = transpose_x(2)
+        scale_x(2, b, [0, 1])
+        quant_x(2, [0, 1])
+        gate_mm(0, by_bank[4:])
+        stats(0)
+        weigh_o_v(0, NVS[0])
+        weigh_o_g(0, NVS[0], 1)
+        recip(0)
         gate_mm(1, by_bank[:GM1])
         for c in range(4):
             gate_mul(0, c)
         stats(1)
-        weigh_o(1, NVS[1])
-        scale_x(2, b, [0, 1])
-        quant_x(2, [0, 1])
+        weigh_o_v(1, NVS[1])
+        weigh_o_g(1, NVS[1], GH1)
         cast_x(3)
         recip(1)
+        weigh_o_g(2, NVS[2], GH1)
         for k in range(0, NT + 1):
             if 0 <= k - 2 < NT:
                 store(k - 2, 1)
@@ -329,11 +348,12 @@ def tile_multiscaleretention_pc_w4_kernel(
                 gate_mm(k + 1, by_bank[GM1:] if k == 0 else by_bank)
                 for c in range(4):
                     gate_mul(k + 1, c)
+            if k + 2 < NT:
+                weigh_o_v(k + 2, NVS[k + 2])
             if 0 <= k < NT and k < SE:
                 transpose_h(k)
             if k + 2 < NT:
                 stats(k + 2)
-                weigh_o(k + 2, NVS[k + 2])
             if 0 <= k < NT and k >= SE:
                 transpose_h(k)
             if k + LA < NT:
@@ -345,6 +365,9 @@ def tile_multiscaleretention_pc_w4_kernel(
                 quant_h(k)
             if k + LA < NT and not QX:
                 quant_x(k + LA, [0, 1])
+            if k + 3 < NT:
+                after(xc[k + 3])
+                weigh_o_g(k + 3, NVS[k + 3], GHS)
             if k + LA + 1 < NT:
                 cast_x(k + LA + 1)
             if k + 2 < NT:

from contextlib import ExitStack

import concourse.mybir as mybir
from concourse.masks import make_identity

F32 = mybir.dt.float32
BF16 = mybir.dt.bfloat16
I32 = mybir.dt.int32
U32 = mybir.dt.uint32
U8 = mybir.dt.uint8
E4M3 = mybir.dt.float8_e4m3fn
FP8X4 = mybir.dt.float8_e4m3fn_x4
FP4X4 = mybir.dt.float4_e2m1fn_x4
ACT = mybir.ActivationFunctionType
ALU = mybir.AluOpType

T, E, H, DV = 1024, 1024, 4, 512
F = H * DV
P = 128
NT = T // P
GX = E // 512
GH = F // 512
EPS = 1e-5
GCOLS = 256
NVS = [1,1,1,1,1,1,1,1]
GM1 = 4
QX = 0
LA = 3
SPOS = 9
RPOS = 9
CV = (0,)
CH = (1,)
SE = 1
N1S = 1
GHS = 1
GH1 = 1
FLOPS = 2 * T * E * F * 2
BYTES = T * F * 2 + T * E + E * 4 + 2 * (E * F // 2 + E * F // 32) + DV * 2 + T * E * 4


def tile_multiscaleretention_pc_w4_kernel(
    tc, o_ret, x_bytes, x_scale, Wg_words, Wg_scales, gn_weight, Wo_words, Wo_scales, out
):
    nc = tc.nc
    o_view = o_ret.rearrange("b (p i) h d -> i p (b h d)", i=NT)
    x_view = x_bytes.rearrange("b (p i) e -> p (b i) e", i=NT)
    out_view = out.rearrange("b (p i) e -> i p (b e)", i=NT)

    with ExitStack() as ctx:
        const = ctx.enter_context(tc.tile_pool(name="const", bufs=1))
        xpool = ctx.enter_context(tc.tile_pool(name="xpool", bufs=6))
        hpool = ctx.enter_context(tc.tile_pool(name="hpool", bufs=2))
        opool = ctx.enter_context(tc.tile_pool(name="opool", bufs=3))
        psum = ctx.enter_context(tc.psum_pool(name="psum", bufs=7))
        wpsum = ctx.enter_context(tc.psum_pool(name="wpsum", bufs=1))

        wg_sc = const.tile([P, GX, F], U8, name="wg_sc", align_bytes=64)
        wo_sc = const.tile([P, GH, E], U8, name="wo_sc", align_bytes=64)
        nc.vector.memset(wg_sc[:].rearrange("p g n -> p (g n)").bitcast(I32), 0)
        ident = const.tile([P, P], F32, name="ident")
        make_identity(nc, ident[:])
        nc.vector.memset(wo_sc[:].rearrange("p g n -> p (g n)").bitcast(I32), 0)

        ctx.enter_context(tc.manual_schedule())

        x_cuts = [(0, 1), (1, 4), (4, 8)]
        x_tiles = [
            const.tile([P, b - a, E], U8, name="xbytes%d" % a) for a, b in x_cuts
        ]
        o_tiles = [const.tile([P, F], BF16, name="o%d" % i) for i in range(NT)]
        wg = [const.tile([P, GX, F], U8, name="wg%d" % k, align_bytes=64) for k in range(2)]
        wo = [const.tile([P, 2, 2 * E], U8, name="wo%d" % k, align_bytes=64) for k in range(2)]
        s4 = const.tile([P, GX, 4], F32, name="s4")
        gnw = const.tile([P, DV], BF16, name="gnw")
        w4 = const.tile([P, 4], BF16, name="w4")
        identb = const.tile([P, P], BF16, name="identb")
        nc.vector.tensor_copy(out=identb[:], in_=ident[:])

        def load_x(k):
            a, b = x_cuts[k]
            nc.sync.dma_start(out=x_tiles[k][:], in_=x_view[:, a:b, :])

        def load_scales(sc, hbm):
            for r in range(4):
                nc.sync.dma_start(
                    out=sc[r:P:32, :, :].rearrange("q g n -> q g n").bitcast(I32),
                    in_=hbm[:, r:16:4, :].rearrange("g q n -> q g n").bitcast(I32),
                )

        def load_o(i):
            nc.sync.dma_start(out=o_tiles[i][:], in_=o_view[i])

        wg_v = Wg_words.rearrange("g p n -> p g n")
        wo_v = Wo_words.rearrange("g p n -> p g n")
        wg_v = Wg_words.rearrange("g p n -> p g n")
        wo_v = Wo_words.rearrange("g p n -> p g n")
        load_x(0)
        nc.sync.dma_start(out=s4[:], in_=x_scale.rearrange("a b (g p t) -> p (a b g) t", p=P, t=4))
        nc.sync.dma_start(out=w4[:], in_=gn_weight.rearrange("(p t) -> p t", t=4))
        load_x(1)
        load_scales(wg_sc, Wg_scales)
        nc.sync.dma_start(out=wg[0][:], in_=wg_v[:, :, 0:F])
        load_o(0)
        nc.sync.dma_start(out=wg[1][:], in_=wg_v[:, :, F : 2 * F])
        load_o(1)
        load_x(2)
        load_o(2)
        load_scales(wo_sc, Wo_scales)
        nc.sync.dma_start(out=wo[0][:], in_=wo_v[:, 0:2, :])
        nc.sync.dma_start(out=wo[1][:], in_=wo_v[:, 2:4, :])
        load_o(3)
        load_o(4)
        load_o(5)
        load_o(6)
        load_o(7)

        xb, xs, xc, xsc = {}, {}, {}, {}
        ss, rr, ow, hb, hs, hc, hsc = {}, {}, {}, {}, {}, {}, {}

        def bank(name):
            return psum.tile([P, 512], F32, name=name, tag="bank")

        def x_src(i):
            for k, (a, b) in enumerate(x_cuts):
                if a <= i < b:
                    return x_tiles[k][:, i - a, :]

        def cast_x(i):
            xb[i] = xpool.tile([P, E], BF16, name="xb", tag="xb", align_bytes=64)
            src = x_src(i)
            nc.scalar.copy(out=xb[i][:, 0:512], in_=src[:, 0:512].bitcast(E4M3))
            if i not in CV:
                nc.scalar.copy(out=xb[i][:, 512:1024], in_=src[:, 512:1024].bitcast(E4M3))
            else:
                nc.vector.tensor_copy(out=xb[i][:, 512:1024], in_=src[:, 512:1024].bitcast(E4M3))

        def transpose_x(i):
            b = bank("xt")
            words = xb[i][:].bitcast(F32)
            for g in range(GX):
                for u in range(2):
                    j = 2 * u + g
                    nc.tensor.transpose(
                        b[:, P * j : P * (j + 1)], words[:, 256 * g + u : 256 * (g + 1) : 2], ident[:]
                    )
            return b

        def scale_x(i, b, passes):
            if passes[0] == 0:
                xs[i] = xpool.tile([P, GX, P, 4], BF16, name="xs", tag="xs", align_bytes=64)
            g0, g1 = passes[0], passes[-1] + 1
            src = b[:].bitcast(BF16).rearrange("p (u g n e) -> p g n u e", u=2, g=GX, e=2)
            nc.vector.tensor_tensor(
                out=xs[i][:, g0:g1].rearrange("p g n (u e) -> p g n u e", u=2),
                in0=src[:, g0:g1],
                in1=s4[:, g0:g1, :]
                .rearrange("p g (u e) -> p g u e", u=2)
                .unsqueeze(2)
                .to_broadcast([P, g1 - g0, P, 2, 2]),
                op=ALU.mult,
            )

        def quant_x(i, passes):
            if passes[0] == 0:
                xc[i] = xpool.tile([P, GX * P], U32, name="xc", tag="xc", align_bytes=64)
                xsc[i] = xpool.tile([P, GX * P], U8, name="xsc", tag="xsc", align_bytes=64)
            w = slice(P * passes[0], P * (passes[-1] + 1))
            nc.vector.quantize_mx(
                out=xc[i][:, w].bitcast(FP8X4),
                scales=xsc[i][:, w],
                in_=xs[i][:, passes[0] : passes[-1] + 1].rearrange("p g n t -> p (g n t)"),
            )

        def stats(i):
            ss[i] = hpool.tile([P, H], F32, name="ss", tag="ss")
            for h in range(H):
                src = o_tiles[i][:, DV * h : DV * (h + 1)]
                junk = hpool.tile([P, DV], BF16, name="junk", tag="junk")
                nc.scalar.activation(out=junk[:], in_=src, func=ACT.Square, accum_out=ss[i][:, h : h + 1])
            rr[i] = hpool.tile([P, H], F32, name="rr", tag="rr")
            nc.scalar.activation(
                out=rr[i][:], in_=ss[i][:], func=ACT.Abs_reciprocal_sqrt, scale=1.0 / DV, bias=EPS
            )

        def recip(i):
            pass

        wb = wpsum.tile([P, DV], BF16, name="wb")

        def spread_w():
            for t in range(4):
                nc.tensor.transpose(
                    wb[:, P * t : P * (t + 1)], w4[:, t : t + 1].to_broadcast([P, P]), identb[:]
                )
            nc.scalar.copy(
                out=gnw[:].rearrange("p (n t) -> p n t", t=4),
                in_=wb[:].rearrange("p (t n) -> p n t", t=4),
            )

        def alloc_ow(i):
            if i not in ow:
                ow[i] = opool.tile([P, F], F32, name="ow", tag="ow")

        def weigh_o_v(i, n_vector):
            alloc_ow(i)
            for h in range(n_vector):
                cols = slice(DV * h, DV * (h + 1))
                nc.vector.tensor_tensor(
                    out=ow[i][:, cols].rearrange("p (n t) -> p n t", t=4),
                    in0=o_tiles[i][:, cols].rearrange("p (n t) -> p n t", t=4),
                    in1=wb[:].rearrange("p (t n) -> p n t", t=4),
                    op=ALU.mult,
                )

        def weigh_o_g(i, n_vector, heads):
            alloc_ow(i)
            for h in range(n_vector, H, heads):
                n = min(heads, H - h)
                cols = slice(DV * h, DV * (h + n))
                nc.gpsimd.tensor_tensor(
                    out=ow[i][:, cols],
                    in0=o_tiles[i][:, cols],
                    in1=gnw[:],
                    op=ALU.mult,
                )

        def after(tile):
            token = hpool.tile([P, 1], U32, name="token", tag="token")
            nc.gpsimd.tensor_copy(out=token[:], in_=tile[:, 0:1])

        gb = {}

        def gate_mm(i, order):
            for c, g in order:
                if g == 0:
                    gb[i, c] = bank("g")
                nc.tensor.matmul_mx(
                    out=gb[i, c][:],
                    lhsT=xc[i][:, P * g : P * (g + 1)].bitcast(FP8X4),
                    lhsT_scale=xsc[i][:, P * g : P * (g + 1)],
                    rhs=wg[c // 2][:, g, 1024 * (c % 2) : 1024 * (c % 2) + 1024].bitcast(FP4X4),
                    rhs_scale=wg_sc[:, g, 512 * c : 512 * (c + 1)],
                    start=(g == 0),
                    stop=(g == GX - 1),
                )

        def gate_mul(i, c):
            if c == 0:
                hb[i] = hpool.tile([P, GH, 2, 256], BF16, name="hb", tag="hb", align_bytes=64)
            gv = gb[i, c][:].rearrange("p (n u e) -> p u n e", u=2, e=2)
            wv = ow[i][:, 512 * c : 512 * (c + 1)].rearrange("p (n u e) -> p u n e", u=2, e=2)
            for u in range(2):
                nc.vector.scalar_tensor_tensor(
                    out=hb[i][:, c, u].rearrange("p (n e) -> p n e", e=2),
                    in0=gv[:, u],
                    scalar=rr[i][:, c : c + 1],
                    in1=wv[:, u],
                    op0=ALU.mult,
                    op1=ALU.mult,
                )

        def transpose_h(i):
            hs[i] = hpool.tile([P, GH, P, 4], BF16, name="hs", tag="hs", align_bytes=64)
            words = hb[i][:].rearrange("p g u n -> p (g u n)").bitcast(F32)
            dst = hs[i][:].rearrange("p g n t -> p (g n t)").bitcast(F32)
            for half in range(2):
                b = bank("ht")
                for j in range(4):
                    k = 4 * half + j
                    nc.tensor.transpose(b[:, P * j : P * (j + 1)], words[:, P * k : P * (k + 1)], ident[:])
                nc.scalar.copy(
                    out=dst[:, 512 * half : 512 * (half + 1)].rearrange("p (g n u) -> p g n u", g=2, u=2),
                    in_=b[:].rearrange("p (g u n) -> p g n u", g=2, u=2),
                )

        def quant_h(i):
            hc[i] = hpool.tile([P, GH * P], U32, name="hc", tag="hc", align_bytes=64)
            hsc[i] = hpool.tile([P, GH * P], U8, name="hsc", tag="hsc", align_bytes=64)
            nc.vector.quantize_mx(
                out=hc[i][:].bitcast(FP8X4),
                scales=hsc[i][:],
                in_=hs[i][:].rearrange("p g n t -> p (g n t)"),
            )

        acc = {}

        def project_mm(i, n):
            acc[i, n] = bank("acc")
            for g in range(GH):
                nc.tensor.matmul_mx(
                    out=acc[i, n][:],
                    lhsT=hc[i][:, P * g : P * (g + 1)].bitcast(FP8X4),
                    lhsT_scale=hsc[i][:, P * g : P * (g + 1)],
                    rhs=wo[g // 2][:, g % 2, E * n : E * (n + 1)].bitcast(FP4X4),
                    rhs_scale=wo_sc[:, g, 512 * n : 512 * (n + 1)],
                    start=(g == 0),
                    stop=(g == GH - 1),
                )

        def store(i, n):
            b = acc[i, n]
            res = opool.tile([P, 512], F32, name="res%d" % n, tag="res%d" % n)
            if n == 0 or (N1S and i < NT - 1):
                nc.scalar.copy(out=res[:], in_=b[:])
            elif i == NT - 1:
                nc.scalar.copy(out=res[:, 0:256], in_=b[:, 0:256])
                nc.vector.tensor_copy(out=res[:, 256:512], in_=b[:, 256:512])
            else:
                nc.vector.tensor_copy(out=res[:], in_=b[:])
            nc.sync.dma_start(out=out_view[i][:, 512 * n : 512 * (n + 1)], in_=res[:])

        by_bank = [(c, g) for c in range(4) for g in range(GX)]
        by_pass = [(c, g) for g in range(GX) for c in range(4)]

        cast_x(0)
        b = transpose_x(0)
        for g in range(GX):
            scale_x(0, b, [g])
            quant_x(0, [g])
        spread_w()
        cast_x(1)
        b = transpose_x(1)
        scale_x(1, b, [0, 1])
        quant_x(1, [0, 1])
        gate_mm(0, by_bank[:4])
        cast_x(2)
        b = transpose_x(2)
        scale_x(2, b, [0, 1])
        quant_x(2, [0, 1])
        gate_mm(0, by_bank[4:])
        stats(0)
        weigh_o_v(0, NVS[0])
        weigh_o_g(0, NVS[0], 1)
        recip(0)
        gate_mm(1, by_bank[:GM1])
        for c in range(4):
            gate_mul(0, c)
        stats(1)
        weigh_o_v(1, NVS[1])
        weigh_o_g(1, NVS[1], GH1)
        cast_x(3)
        recip(1)
        weigh_o_g(2, NVS[2], GH1)
        for k in range(0, NT + 1):
            if 0 <= k - 2 < NT:
                store(k - 2, 1)
            if k + 1 < NT:
                gate_mm(k + 1, by_bank[GM1:] if k == 0 else by_bank)
                for c in range(4):
                    gate_mul(k + 1, c)
            if k + 2 < NT:
                weigh_o_v(k + 2, NVS[k + 2])
            if 0 <= k < NT and k < SE:
                transpose_h(k)
            if k + 2 < NT:
                stats(k + 2)
            if 0 <= k < NT and k >= SE:
                transpose_h(k)
            if k + LA < NT:
                bx = transpose_x(k + LA)
                scale_x(k + LA, bx, [0, 1])
                if QX:
                    quant_x(k + LA, [0, 1])
            if 0 <= k < NT:
                quant_h(k)
            if k + LA < NT and not QX:
                quant_x(k + LA, [0, 1])
            if k + 3 < NT:
                after(xc[k + 3])
                weigh_o_g(k + 3, NVS[k + 3], GHS)
            if k + LA + 1 < NT:
                cast_x(k + LA + 1)
            if k + 2 < NT:
                recip(k + 2)
            if 0 <= k - 1 < NT:
                project_mm(k - 1, 0)
                store(k - 1, 0)
                project_mm(k - 1, 1)
        store(NT - 1, 1)
